import numpy as np
import ml_dtypes


def mxq(x, axis, fmt="e4m3"):
    dtype, down = {"e4m3": (ml_dtypes.float8_e4m3fn, 7), "e5m2": (ml_dtypes.float8_e5m2, 14)}[fmt]
    v = np.moveaxis(np.asarray(x, np.float32).astype(ml_dtypes.bfloat16).astype(np.float64), axis, -1)
    blocks = v.reshape(v.shape[:-1] + (-1, 32))
    amax = np.abs(blocks).max(-1, keepdims=True)
    byte = np.maximum(np.where(amax > 0, np.frexp(amax)[1] - 1 + 127, 0) - down, 1)
    scale = np.exp2(byte - 127.0)
    codes = (blocks / scale).astype(np.float32).astype(dtype).astype(np.float64)
    return np.moveaxis((codes * scale).reshape(v.shape), -1, axis)


WIDE = False


def mx_kscale(k):
    if not WIDE:
        return np.ones(k)
    levels = np.array([10, -10, 5, -5, 0])
    if k % 512:
        return np.exp2(np.random.permutation(np.resize(levels, k // 32))).repeat(32)
    a = np.empty((k // 512, 16))
    for p in range(k // 512):
        a[p, :8] = np.random.permutation(np.resize(levels, 8))
        for g in range(8):
            far = levels[np.abs(levels - a[p, g]) >= 10]
            a[p, g + 8] = far[np.random.randint(len(far))]
    return np.exp2(a.ravel()).repeat(32)


BF16 = ml_dtypes.bfloat16


def bf(x):
    return np.asarray(x, np.float32).astype(BF16)


def f64(x):
    return np.asarray(x).astype(np.float64)


B, S, H, A, NH = 4, 128, 1536, 1536, 12
HD = A // NH
LN_EPS = 1e-5


def setup_inputs():
    s = mx_kscale(A)
    return {"ctx_heads": bf(np.random.standard_normal((B, NH, S, HD)) * s.reshape(NH, 1, HD)),
            "Wo": bf(np.random.standard_normal((H, A)) / np.sqrt(A) / s),
            "bo": bf(np.random.standard_normal(H) * 0.3),
            "features": bf(np.random.standard_normal((B, S, H))),
            "ln_g": bf(1.0 + 0.1 * np.random.standard_normal(H)),
            "ln_b": bf(0.2 * np.random.standard_normal(H))}


def core(ctx_heads, Wo, bo, features, ln_g, ln_b):
    ctx = f64(ctx_heads).transpose(0, 2, 1, 3).reshape(B, S, A)
    p = (mxq(ctx, 2, "e4m3") @ mxq(f64(Wo), 1, "e4m3").T) + f64(bo)
    y = p + f64(features)
    mu = y.mean(-1, keepdims=True)
    var = y.var(-1, keepdims=True)
    return (y - mu) / np.sqrt(var + LN_EPS) * f64(ln_g) + f64(ln_b)


def e4m3fn_bytes(y):
    return np.clip(np.asarray(y, np.float64), -448.0, 448.0).astype(np.float32).astype(ml_dtypes.float8_e4m3fn).view(np.uint8)


def reference(ctx_heads, Wo, bo, features, ln_g, ln_b):
    out = core(ctx_heads, Wo, bo, features, ln_g, ln_b)
    s = np.max(np.abs(out), axis=-1, keepdims=True) / 448.0
    return out, e4m3fn_bytes(out / s)

@@ -1,0 +1,368 @@
+from contextlib import ExitStack
+
+import concourse.masks as masks
+import concourse.mybir as mybir
+
+F32 = mybir.dt.float32
+BF16 = mybir.dt.bfloat16
+U32 = mybir.dt.uint32
+U8 = mybir.dt.uint8
+FP8X4 = mybir.dt.float8_e4m3fn_x4
+FP8 = mybir.dt.float8_e4m3fn
+ALU = mybir.AluOpType
+ACT = mybir.ActivationFunctionType
+AX = mybir.AxisListType
+RSFUNC = ACT.Abs_reciprocal_sqrt
+
+P = 128
+NB = 4
+K = 1536
+N = 1536
+G = 3
+CW = 512
+QW = 256
+EPS = 1e-5
+
+FLOPS = 2 * 512 * 1536 * 1536
+
+
+def tile_hierarchicalattention_pb_kernel(tc, ctx_heads, Wo, bo, features, ln_g, ln_b, out_0, out_1):
+    nc = tc.nc
+    with ExitStack() as es:
+        keep = es.enter_context(tc.tile_pool(name="keep", bufs=1))
+        gp = es.enter_context(tc.tile_pool(name="gp", bufs=6))
+        work = es.enter_context(tc.tile_pool(name="work", bufs=2))
+        op = es.enter_context(tc.tile_pool(name="op", bufs=3))
+        tp = es.enter_context(tc.psum_pool(name="tp", bufs=1))
+        accp = es.enter_context(tc.psum_pool(name="accp", bufs=1))
+        es.enter_context(tc.manual_schedule())
+
+        vr = keep.tile([P, P], BF16, name="vr")
+        nc.vector.memset(vr[:], 0.0)
+        xrows = keep.tile([P, N], BF16, name="xrows")
+        nc.vector.memset(xrows[:], 0.0)
+        onecol = keep.tile([P, 1], F32, name="onecol")
+        nc.vector.memset(onecol[:], 1.0)
+        zcol = keep.tile([P, 1], F32, name="zcol")
+        nc.vector.memset(zcol[:], 0.0)
+        warm = keep.tile([P, 1], F32, name="warm")
+        nc.scalar.activation(out=warm[:], in_=onecol[:], func=RSFUNC)
+
+        ident_b = keep.tile([P, P], BF16, name="ident_b")
+        masks.make_identity(nc, ident_b[:])
+        ident_f = keep.tile([P, P], F32, name="ident_f")
+        masks.make_identity(nc, ident_f[:])
+        lm = [keep.tile([P, P], F32, name="lm%d" % m) for m in range(NB)]
+        for m in range(NB):
+            nc.gpsimd.memset(lm[m][:], 0.0)
+            nc.gpsimd.memset(lm[m][:, 1:2], 1.0)
+
+        wo_raw = [keep.tile([P, 2, K], BF16, name="wo_raw%d" % q) for q in range(6)]
+        ctx_raw = [keep.tile([P, 2, K], BF16, name="ctx_raw%d" % q) for q in range(2)]
+        fc0 = keep.tile([P, NB, CW], BF16, name="fc0")
+        fl = [keep.tile([P, 2, 2 * CW], BF16, name="fl%d" % i) for i in range(2)]
+
+        def load_w(q):
+            nc.sync.dma_start(out=wo_raw[q][:], in_=Wo[2 * P * q:2 * P * (q + 1), :].rearrange("(i p) k -> p i k", i=2))
+
+        def load_x(q):
+            nc.sync.dma_start(out=ctx_raw[q][:].rearrange("p i (h d) -> p (i h) d", d=128), in_=ctx_heads[2 * q:2 * q + 2].rearrange("b h s d -> s (b h) d"))
+
+        def load_f0():
+            nc.sync.dma_start(out=fc0[:], in_=features[:, :, 0:CW].rearrange("b s n -> s b n"))
+
+        def load_fl(i):
+            nc.sync.dma_start(out=fl[i][:], in_=features[2 * i:2 * i + 2, :, CW:N].rearrange("b s n -> s b n"))
+
+        load_w(0)
+        load_x(0)
+        nc.sync.dma_start(out=vr[0:12, :], in_=bo.rearrange("(c j) -> c j", c=12))
+        load_f0()
+        load_w(1)
+        load_x(1)
+        nc.sync.dma_start(out=xrows[0:1, :], in_=ln_g.rearrange("(o n) -> o n", o=1))
+        nc.sync.dma_start(out=xrows[1:2, :], in_=ln_b.rearrange("(o n) -> o n", o=1))
+        load_w(2)
+        load_fl(0)
+        load_w(3)
+        load_w(4)
+        load_w(5)
+        load_fl(1)
+        x32 = keep.tile([P, N], F32, name="x32")
+
+        wo_words = [wo_raw[r // 2][:, r % 2, :].bitcast(F32) for r in range(12)]
+        ctx_words = [ctx_raw[b // 2][:, b % 2, :].bitcast(F32) for b in range(NB)]
+
+        wo_codes = keep.tile([P, G, N], U32, name="wo_codes", align_bytes=64)
+        wo_scales = keep.tile([P, G, N], U8, name="wo_scales", align_bytes=64)
+        cx_codes = keep.tile([P, G, 512], U32, name="cx_codes", align_bytes=64)
+        cx_scales = keep.tile([P, G, 512], U8, name="cx_scales", align_bytes=64)
+
+        vt = keep.tile([P, P], BF16, name="vt")
+        vec_b = keep.tile([P, 2 * N], BF16, name="vec_b")
+        bo_b = vec_b[:, 0:N]
+        g_b = vec_b[:, N:2 * N]
+        nc.sync.dma_start(out=g_b, in_=ln_g.partition_broadcast(P))
+
+        fb = [keep.tile([P, N], F32, name="fb%d" % m) for m in range(NB)]
+        y = [keep.tile([P, N], F32, name="y%d" % m) for m in range(NB)]
+        yg = [keep.tile([P, N], F32, name="yg%d" % m) for m in range(NB)]
+        sums = keep.tile([P, NB, 4], F32, name="sums")
+        sst = keep.tile([P, NB, 8], F32, name="sst")
+        vst = keep.tile([P, NB, 4], F32, name="vst")
+        epscol = keep.tile([P, 1], F32, name="epscol")
+        nc.vector.memset(epscol[:], EPS)
+
+        def cols(c):
+            return slice(c * CW, (c + 1) * CW)
+
+        def spread(v):
+            for first, count, bank in ((0, 8, 2 * v), (8, 4, 2 * v + 1)):
+                ps = accp.tile([P, 1024], BF16, name="a%d" % bank, tag="a%d" % bank)
+                for j in range(count):
+                    i = 12 * v + first + j
+                    nc.tensor.transpose(ps[:, j * P:(j + 1) * P], vt[:, i:i + 1].to_broadcast([P, P]), ident_b[:])
+                nc.scalar.copy(out=vec_b[:, v * N + first * P:v * N + (first + count) * P], in_=ps[:, 0:count * P])
+
+        unit_no = [0]
+
+        def run_t(words2, vset):
+            res = []
+            for g in range(G):
+                xt = tp.tile([P, 2, 2, P], F32, name="t%d" % (unit_no[0] % 4), tag="t%d" % (unit_no[0] % 4))
+                unit_no[0] += 1
+                for i in range(2):
+                    for u in range(2):
+                        nc.tensor.transpose(xt[:, i, u, :], words2[i][:, 256 * g + u:256 * (g + 1):2], ident_f[:])
+                grouped = gp.tile([P, 1024], BF16, name="grouped", align_bytes=64)
+                copy = nc.vector.tensor_copy if g in vset else nc.scalar.copy
+                copy(out=grouped[:].bitcast(F32).rearrange("p (i n u) -> p i n u", i=2, u=2), in_=xt[:].rearrange("p i u n -> p i n u"))
+                res.append(grouped)
+            return res
+
+        def run_w(q, vset=()):
+            return run_t((wo_words[2 * q], wo_words[2 * q + 1]), vset)
+
+        def run_x(q, vset=()):
+            return run_t((ctx_words[2 * q], ctx_words[2 * q + 1]), vset)
+
+        def qw(res, q, g):
+            nc.vector.quantize_mx(out=wo_codes[:, g, QW * q:QW * (q + 1)].bitcast(FP8X4), scales=wo_scales[:, g, QW * q:QW * (q + 1)], in_=res[g][:])
+
+        def qx(res, q, g):
+            nc.vector.quantize_mx(out=cx_codes[:, g, QW * q:QW * (q + 1)].bitcast(FP8X4), scales=cx_scales[:, g, QW * q:QW * (q + 1)], in_=res[g][:])
+
+        acc = {}
+
+        def bank(m, c):
+            return m if c == 0 else (2 * m + c - 1) % 4
+
+        def mm(q, m):
+            c = q // 2
+            h = q % 2
+            if h == 0:
+                acc[(m, c)] = accp.tile([P, CW], F32, name="a%d" % bank(m, c), tag="a%d" % bank(m, c))
+            for g in range(G):
+                nc.tensor.matmul_mx(
+                    out=acc[(m, c)][:, h * QW:(h + 1) * QW],
+                    lhsT=cx_codes[:, g, P * m:P * (m + 1)].bitcast(FP8X4),
+                    lhsT_scale=cx_scales[:, g, P * m:P * (m + 1)],
+                    rhs=wo_codes[:, g, QW * q:QW * (q + 1)].bitcast(FP8X4),
+                    rhs_scale=wo_scales[:, g, QW * q:QW * (q + 1)],
+                    start=(g == 0),
+                    stop=(g == G - 1),
+                )
+
+        def p0(eng, m, lo, hi):
+            src = fc0[:, m, :] if lo == 0 else fl[m // 2][:, m % 2, lo - CW:hi - CW]
+            eng.tensor_tensor(out=fb[m][:, lo:hi], in0=src, in1=bo_b[:, lo:hi], op=ALU.add)
+
+        def p1(m, c):
+            nc.vector.scalar_tensor_tensor(out=y[m][:, cols(c)], in0=acc[(m, c)][:], scalar=1.0, in1=fb[m][:, cols(c)], op0=ALU.mult, op1=ALU.add, accum_out=sums[:, m, c:c + 1])
+
+        def p2(m, lo, hi):
+            nc.gpsimd.tensor_tensor(out=yg[m][:, lo:hi], in0=y[m][:, lo:hi], in1=g_b[:, lo:hi], op=ALU.mult)
+
+        def stats(m):
+            negmean = sst[:, m, 3:4]
+            nc.scalar.activation(out=sst[:, m, 0:3], in_=sums[:, m, 0:3], func=ACT.Copy, scale=-1.0 / N, accum_out=negmean)
+            junk = work.tile([P, N], BF16, name="junk")
+            nc.scalar.activation(out=junk[:], in_=y[m][:], func=ACT.Square, bias=negmean, scale=1.0, accum_out=sst[:, m, 4:5])
+            nc.scalar.activation(out=sst[:, m, 5:6], in_=sst[:, m, 4:5], func=RSFUNC, bias=epscol[:, 0:1], scale=1.0 / N)
+            nc.scalar.activation(out=lm[m][:, 0:1], in_=negmean, func=ACT.Copy, scale=sst[:, m, 5:6])
+
+        lt_ps = {}
+        lt_sb = {}
+        r_ps = {}
+        o = {}
+
+        R_BANKS = ((tp, "t1"), (tp, "t2"), (tp, "t3"), (accp, "a0"), (accp, "a1"), (accp, "a2"), (accp, "a3"))
+
+        def pt(m):
+            if m == 0:
+                lt_ps[0] = tp.tile([P, NB, P], F32, name="t0", tag="t0")
+            nc.tensor.transpose(lt_ps[0][:, m, :], lm[m][:], ident_f[:])
+
+        def sl(m, eng_copy):
+            lt_sb[m] = keep.tile([P, P], F32, name="lt_sb%d" % m)
+            eng_copy(out=lt_sb[m][:], in_=lt_ps[0][:, m, :])
+
+        def pr(m):
+            for c in range(3):
+                pool, tag = R_BANKS[(3 * m + c) % 7]
+                r_ps[(m, c)] = pool.tile([P, CW], F32, name=tag, tag=tag)
+                nc.tensor.matmul(out=r_ps[(m, c)][:], lhsT=lt_sb[m][:], rhs=x32[:, cols(c)], start=True, stop=True)
+
+        def bb(m, c):
+            if c == 0:
+                o[m] = op.tile([P, N], F32, name="o")
+            nc.vector.scalar_tensor_tensor(out=o[m][:, cols(c)], in0=yg[m][:, cols(c)], scalar=sst[:, m, 5:6], in1=r_ps[(m, c)][:], op0=ALU.mult, op1=ALU.add)
+            nc.sync.dma_start(out=out_0[m][:, cols(c)], in_=o[m][:, cols(c)])
+
+        def ca(m):
+            nc.vector.tensor_reduce(out=vst[:, m, 0:1], in_=o[m][:], axis=AX.X, op=ALU.max, apply_absolute_value=True)
+
+        def rc(m):
+            nc.vector.reciprocal(out=vst[:, m, 1:2], in_=vst[:, m, 0:1])
+
+        def rr(m):
+            nc.vector.tensor_scalar(out=vst[:, m, 2:3], in0=vst[:, m, 1:2], scalar1=448.0, scalar2=None, op0=ALU.mult)
+
+        def kk(m, split):
+            o8 = work.tile([P, N], FP8, name="o8")
+            nc.scalar.activation(out=o8[:, 0:split], in_=o[m][:, 0:split], func=ACT.Identity, scale=vst[:, m, 2:3], bias=zcol[:, 0:1], saturate=False)
+            if split < N:
+                nc.vector.tensor_scalar(out=o8[:, split:N], in0=o[m][:, split:N], scalar1=vst[:, m, 2:3], scalar2=None, op0=ALU.mult, saturate=False)
+            nc.sync.dma_start(out=out_1[m], in_=o8[:].bitcast(U8))
+
+        V = nc.vector
+        GP = nc.gpsimd
+        res = run_w(0, (1,))
+        for g in range(G):
+            qw(res, 0, g)
+        res = run_x(0, (1,))
+        for g in range(G):
+            qx(res, 0, g)
+        vt_ps = tp.tile([P, P], BF16, name="t%d" % (unit_no[0] % 4), tag="t%d" % (unit_no[0] % 4))
+        unit_no[0] += 1
+        nc.tensor.transpose(vt_ps[:], vr[:], ident_b[:])
+        nc.scalar.copy(out=vt[:], in_=vt_ps[:])
+        spread(0)
+        res = run_w(1, (1,))
+        p0(V, 0, 0, CW)
+        p0(V, 1, 0, CW)
+        qw(res, 1, 0)
+        p0(V, 2, 0, CW)
+        qw(res, 1, 1)
+        p0(V, 3, 0, CW)
+        qw(res, 1, 2)
+        mm(0, 0)
+        mm(0, 1)
+        res = run_x(1, (1,))
+        for g in range(G):
+            qx(res, 1, g)
+        mm(1, 0)
+        mm(1, 1)
+        for m in (0, 1):
+            p1(m, 0)
+        res = run_w(2, ())
+        for g in range(G):
+            qw(res, 2, g)
+        mm(0, 2)
+        mm(0, 3)
+        res = run_w(3, ())
+        for g in range(G):
+            qw(res, 3, g)
+        mm(1, 2)
+        mm(1, 3)
+        for m in (2, 3):
+            p1(m, 0)
+        p0(V, 0, CW, N)
+        res = run_w(4, ())
+        for g in range(G):
+            qw(res, 4, g)
+        p0(V, 1, CW, N)
+        res = run_w(5, ())
+        for g in range(G):
+            qw(res, 5, g)
+        nc.scalar.copy(out=x32[:], in_=xrows[:])
+        for m in (2, 3):
+            p0(GP, m, CW, 2 * CW)
+            p0(GP, m, 2 * CW, N)
+
+        def p2all(m):
+            for c in (0, 1, 2):
+                p2(m, c * CW, (c + 1) * CW)
+
+        def pr1(m, c):
+            pool, tag = R_BANKS[(3 * m + c) % 7]
+            r_ps[(m, c)] = pool.tile([P, CW], F32, name=tag, tag=tag)
+            nc.tensor.matmul(out=r_ps[(m, c)][:], lhsT=lt_sb[m][:], rhs=x32[:, cols(c)], start=True, stop=True)
+
+        for m in (0, 1):
+            mm(2, m)
+            mm(3, m)
+            p1(m, 1)
+            mm(4, m)
+        for m in (0, 1):
+            mm(5, m)
+            p1(m, 2)
+            stats(m)
+            p2all(m)
+        for m in (2, 3):
+            mm(2, m)
+            mm(3, m)
+            p1(m, 1)
+            mm(4, m)
+            mm(5, m)
+            if m == 3:
+                pt(0)
+                sl(0, nc.vector.tensor_copy)
+            p1(m, 2)
+        pr1(0, 0)
+        pr1(0, 1)
+        pt(1)
+        sl(1, nc.scalar.copy)
+        pr1(0, 2)
+        stats(2)
+        p2all(2)
+        pr1(1, 0)
+        pr1(1, 1)
+        pt(2)
+        sl(2, nc.scalar.copy)
+        pr1(1, 2)
+        stats(3)
+        p2all(3)
+        for c in range(3):
+            bb(0, c)
+        pr1(2, 0)
+        pr1(2, 1)
+        pt(3)
+        sl(3, nc.scalar.copy)
+        pr1(2, 2)
+        ca(0)
+        bb(1, 0)
+        rc(0)
+        bb(1, 1)
+        rr(0)
+        bb(1, 2)
+        pr(3)
+        kk(0, N)
+        bb(2, 0)
+        ca(1)
+        bb(2, 1)
+        rc(1)
+        bb(2, 2)
+        rr(1)
+        kk(1, N)
+        bb(3, 0)
+        ca(2)
+        bb(3, 1)
+        rc(2)
+        bb(3, 2)
+        rr(2)
+        kk(2, N)
+        ca(3)
+        rc(3)
+        rr(3)
+        kk(3, CW)

@@ -32,63 +32,73 @@ def tile_hierarchicalattention_pb_kernel(tc, ctx_heads, Wo, bo, features, ln_g, 
         keep = es.enter_context(tc.tile_pool(name="keep", bufs=1))
         gp = es.enter_context(tc.tile_pool(name="gp", bufs=6))
         work = es.enter_context(tc.tile_pool(name="work", bufs=2))
-        op = es.enter_context(tc.tile_pool(name="op", bufs=3))
-        tp = es.enter_context(tc.psum_pool(name="tp", bufs=1))
-        accp = es.enter_context(tc.psum_pool(name="accp", bufs=1))
+        op = es.enter_context(tc.tile_pool(name="op", bufs=4))
+        ps = es.enter_context(tc.psum_pool(name="ps", bufs=1))
         es.enter_context(tc.manual_schedule())
 
+        def bank(i, shape, dtype):
+            t = ps.tile(shape, dtype, name="b%d" % i, tag="b%d" % i)
+            return t
+
         vr = keep.tile([P, P], BF16, name="vr")
-        nc.vector.memset(vr[:], 0.0)
+        nc.gpsimd.memset(vr[:], 0.0)
         xrows = keep.tile([P, N], BF16, name="xrows")
         nc.vector.memset(xrows[:], 0.0)
         onecol = keep.tile([P, 1], F32, name="onecol")
         nc.vector.memset(onecol[:], 1.0)
         zcol = keep.tile([P, 1], F32, name="zcol")
         nc.vector.memset(zcol[:], 0.0)
+        epscol = keep.tile([P, 1], F32, name="epscol")
+        nc.vector.memset(epscol[:], EPS)
         warm = keep.tile([P, 1], F32, name="warm")
         nc.scalar.activation(out=warm[:], in_=onecol[:], func=RSFUNC)
 
-        ident_b = keep.tile([P, P], BF16, name="ident_b")
-        masks.make_identity(nc, ident_b[:])
         ident_f = keep.tile([P, P], F32, name="ident_f")
         masks.make_identity(nc, ident_f[:])
-        lm = [keep.tile([P, P], F32, name="lm%d" % m) for m in range(NB)]
+        ident_b = keep.tile([P, P], BF16, name="ident_b")
+        masks.make_identity(nc, ident_b[:])
+        lm = [keep.tile([P, P], BF16, name="lm%d" % m) for m in range(NB)]
         for m in range(NB):
             nc.gpsimd.memset(lm[m][:], 0.0)
-            nc.gpsimd.memset(lm[m][:, 1:2], 1.0)
+            nc.gpsimd.memset(lm[m][:, 4:5], 1.0)
 
         wo_raw = [keep.tile([P, 2, K], BF16, name="wo_raw%d" % q) for q in range(6)]
         ctx_raw = [keep.tile([P, 2, K], BF16, name="ctx_raw%d" % q) for q in range(2)]
-        fc0 = keep.tile([P, NB, CW], BF16, name="fc0")
-        fl = [keep.tile([P, 2, 2 * CW], BF16, name="fl%d" % i) for i in range(2)]
+        f = [keep.tile([P, N], BF16, name="f%d" % m) for m in range(NB)]
+        vec_b = keep.tile([P, 2 * N], BF16, name="vec_b")
+        bo_b = vec_b[:, 0:N]
+        g_b = vec_b[:, N:2 * N]
 
         def load_w(q):
             nc.sync.dma_start(out=wo_raw[q][:], in_=Wo[2 * P * q:2 * P * (q + 1), :].rearrange("(i p) k -> p i k", i=2))
 
+        def load_w_half(q, i):
+            nc.sync.dma_start(out=wo_raw[q][:, i, :], in_=Wo[P * (2 * q + i):P * (2 * q + i + 1), :])
+
         def load_x(q):
             nc.sync.dma_start(out=ctx_raw[q][:].rearrange("p i (h d) -> p (i h) d", d=128), in_=ctx_heads[2 * q:2 * q + 2].rearrange("b h s d -> s (b h) d"))
 
-        def load_f0():
-            nc.sync.dma_start(out=fc0[:], in_=features[:, :, 0:CW].rearrange("b s n -> s b n"))
+        def load_f(m):
+            nc.sync.dma_start(out=f[m][:], in_=features[m])
 
-        def load_fl(i):
-            nc.sync.dma_start(out=fl[i][:], in_=features[2 * i:2 * i + 2, :, CW:N].rearrange("b s n -> s b n"))
-
-        load_w(0)
-        load_x(0)
+        load_w_half(0, 0)
         nc.sync.dma_start(out=vr[0:12, :], in_=bo.rearrange("(c j) -> c j", c=12))
-        load_f0()
+        load_w_half(0, 1)
+        load_x(0)
+        load_f(0)
         load_w(1)
         load_x(1)
-        nc.sync.dma_start(out=xrows[0:1, :], in_=ln_g.rearrange("(o n) -> o n", o=1))
-        nc.sync.dma_start(out=xrows[1:2, :], in_=ln_b.rearrange("(o n) -> o n", o=1))
         load_w(2)
-        load_fl(0)
+        load_f(1)
+        for r in range(3):
+            nc.sync.dma_start(out=xrows[r:r + 1, :], in_=ln_g.rearrange("(o n) -> o n", o=1))
+        nc.sync.dma_start(out=xrows[4:5, :], in_=ln_b.rearrange("(o n) -> o n", o=1))
         load_w(3)
+        load_f(2)
         load_w(4)
         load_w(5)
-        load_fl(1)
-        x32 = keep.tile([P, N], F32, name="x32")
+        load_f(3)
+        nc.sync.dma_start(out=g_b, in_=ln_g.partition_broadcast(P))
 
         wo_words = [wo_raw[r // 2][:, r % 2, :].bitcast(F32) for r in range(12)]
         ctx_words = [ctx_raw[b // 2][:, b % 2, :].bitcast(F32) for b in range(NB)]
@@ -99,52 +109,55 @@ def tile_hierarchicalattention_pb_kernel(tc, ctx_heads, Wo, bo, features, ln_g, 
         cx_scales = keep.tile([P, G, 512], U8, name="cx_scales", align_bytes=64)
 
         vt = keep.tile([P, P], BF16, name="vt")
-        vec_b = keep.tile([P, 2 * N], BF16, name="vec_b")
-        bo_b = vec_b[:, 0:N]
-        g_b = vec_b[:, N:2 * N]
-        nc.sync.dma_start(out=g_b, in_=ln_g.partition_broadcast(P))
-
         fb = [keep.tile([P, N], F32, name="fb%d" % m) for m in range(NB)]
         y = [keep.tile([P, N], F32, name="y%d" % m) for m in range(NB)]
         yg = [keep.tile([P, N], F32, name="yg%d" % m) for m in range(NB)]
         sums = keep.tile([P, NB, 4], F32, name="sums")
         sst = keep.tile([P, NB, 8], F32, name="sst")
         vst = keep.tile([P, NB, 4], F32, name="vst")
-        epscol = keep.tile([P, 1], F32, name="epscol")
-        nc.vector.memset(epscol[:], EPS)
+        sca = keep.tile([P, NB], F32, name="sca")
 
         def cols(c):
             return slice(c * CW, (c + 1) * CW)
 
-        def spread(v):
-            for first, count, bank in ((0, 8, 2 * v), (8, 4, 2 * v + 1)):
-                ps = accp.tile([P, 1024], BF16, name="a%d" % bank, tag="a%d" % bank)
+        def spread():
+            for first, count, b in ((0, 8, 6), (8, 4, 7)):
+                pst = bank(b, [P, 1024], BF16)
                 for j in range(count):
-                    i = 12 * v + first + j
-                    nc.tensor.transpose(ps[:, j * P:(j + 1) * P], vt[:, i:i + 1].to_broadcast([P, P]), ident_b[:])
-                nc.scalar.copy(out=vec_b[:, v * N + first * P:v * N + (first + count) * P], in_=ps[:, 0:count * P])
+                    i = first + j
+                    nc.tensor.transpose(pst[:, j * P:(j + 1) * P], vt[:, i:i + 1].to_broadcast([P, P]), ident_b[:])
+                nc.vector.tensor_copy(out=vec_b[:, first * P:(first + count) * P], in_=pst[:, 0:count * P])
 
+        TB = (0, 1, 2, 3, 4)
         unit_no = [0]
 
-        def run_t(words2, vset):
+        def run_t(words2, by_tile=False):
+            xts = []
+            for g in range(G):
+                xt = bank(TB[unit_no[0] % len(TB)], [P, 2, 2, P], F32)
+                unit_no[0] += 1
+                xts.append(xt)
+                if not by_tile:
+                    for i in range(2):
+                        for u in range(2):
+                            nc.tensor.transpose(xt[:, i, u, :], words2[i][:, 256 * g + u:256 * (g + 1):2], ident_f[:])
+            if by_tile:
+                for i in range(2):
+                    for g in range(G):
+                        for u in range(2):
+                            nc.tensor.transpose(xts[g][:, i, u, :], words2[i][:, 256 * g + u:256 * (g + 1):2], ident_f[:])
             res = []
             for g in range(G):
-                xt = tp.tile([P, 2, 2, P], F32, name="t%d" % (unit_no[0] % 4), tag="t%d" % (unit_no[0] % 4))
-                unit_no[0] += 1
-                for i in range(2):
-                    for u in range(2):
-                        nc.tensor.transpose(xt[:, i, u, :], words2[i][:, 256 * g + u:256 * (g + 1):2], ident_f[:])
                 grouped = gp.tile([P, 1024], BF16, name="grouped", align_bytes=64)
-                copy = nc.vector.tensor_copy if g in vset else nc.scalar.copy
-                copy(out=grouped[:].bitcast(F32).rearrange("p (i n u) -> p i n u", i=2, u=2), in_=xt[:].rearrange("p i u n -> p i n u"))
+                nc.scalar.copy(out=grouped[:].bitcast(F32).rearrange("p (i n u) -> p i n u", i=2, u=2), in_=xts[g][:].rearrange("p i u n -> p i n u"))
                 res.append(grouped)
             return res
 
-        def run_w(q, vset=()):
-            return run_t((wo_words[2 * q], wo_words[2 * q + 1]), vset)
+        def run_w(q, by_tile=False):
+            return run_t((wo_words[2 * q], wo_words[2 * q + 1]), by_tile)
 
-        def run_x(q, vset=()):
-            return run_t((ctx_words[2 * q], ctx_words[2 * q + 1]), vset)
+        def run_x(q):
+            return run_t((ctx_words[2 * q], ctx_words[2 * q + 1]))
 
         def qw(res, q, g):
             nc.vector.quantize_mx(out=wo_codes[:, g, QW * q:QW * (q + 1)].bitcast(FP8X4), scales=wo_scales[:, g, QW * q:QW * (q + 1)], in_=res[g][:])
@@ -153,15 +166,14 @@ def tile_hierarchicalattention_pb_kernel(tc, ctx_heads, Wo, bo, features, ln_g, 
             nc.vector.quantize_mx(out=cx_codes[:, g, QW * q:QW * (q + 1)].bitcast(FP8X4), scales=cx_scales[:, g, QW * q:QW * (q + 1)], in_=res[g][:])
 
         acc = {}
-
-        def bank(m, c):
-            return m if c == 0 else (2 * m + c - 1) % 4
+        ABANK = {(0, 0): 5, (0, 1): 6, (0, 2): 7, (1, 0): 4, (1, 1): 0, (1, 2): 1, (2, 0): 2, (2, 1): 4, (2, 2): 0, (3, 0): 1, (3, 1): 2, (3, 2): 4}
+        RB = (6, 7, 3)
 
         def mm(q, m):
             c = q // 2
             h = q % 2
             if h == 0:
-                acc[(m, c)] = accp.tile([P, CW], F32, name="a%d" % bank(m, c), tag="a%d" % bank(m, c))
+                acc[(m, c)] = bank(ABANK[(m, c)], [P, CW], F32)
             for g in range(G):
                 nc.tensor.matmul_mx(
                     out=acc[(m, c)][:, h * QW:(h + 1) * QW],
@@ -173,45 +185,50 @@ def tile_hierarchicalattention_pb_kernel(tc, ctx_heads, Wo, bo, features, ln_g, 
                     stop=(g == G - 1),
                 )
 
-        def p0(eng, m, lo, hi):
-            src = fc0[:, m, :] if lo == 0 else fl[m // 2][:, m % 2, lo - CW:hi - CW]
-            eng.tensor_tensor(out=fb[m][:, lo:hi], in0=src, in1=bo_b[:, lo:hi], op=ALU.add)
+        def p0(m, lo, hi):
+            nc.vector.tensor_tensor(out=fb[m][:, lo:hi], in0=f[m][:, lo:hi], in1=bo_b[:, lo:hi], op=ALU.add)
 
         def p1(m, c):
             nc.vector.scalar_tensor_tensor(out=y[m][:, cols(c)], in0=acc[(m, c)][:], scalar=1.0, in1=fb[m][:, cols(c)], op0=ALU.mult, op1=ALU.add, accum_out=sums[:, m, c:c + 1])
 
-        def p2(m, lo, hi):
-            nc.gpsimd.tensor_tensor(out=yg[m][:, lo:hi], in0=y[m][:, lo:hi], in1=g_b[:, lo:hi], op=ALU.mult)
+        def p2(m, c):
+            nc.gpsimd.tensor_tensor(out=yg[m][:, cols(c)], in0=y[m][:, cols(c)], in1=g_b[:, cols(c)], op=ALU.mult)
 
-        def stats(m):
+        def st1(m):
             negmean = sst[:, m, 3:4]
             nc.scalar.activation(out=sst[:, m, 0:3], in_=sums[:, m, 0:3], func=ACT.Copy, scale=-1.0 / N, accum_out=negmean)
             junk = work.tile([P, N], BF16, name="junk")
             nc.scalar.activation(out=junk[:], in_=y[m][:], func=ACT.Square, bias=negmean, scale=1.0, accum_out=sst[:, m, 4:5])
-            nc.scalar.activation(out=sst[:, m, 5:6], in_=sst[:, m, 4:5], func=RSFUNC, bias=epscol[:, 0:1], scale=1.0 / N)
-            nc.scalar.activation(out=lm[m][:, 0:1], in_=negmean, func=ACT.Copy, scale=sst[:, m, 5:6])
+
+        def st2(m):
+            negmean = sst[:, m, 3:4]
+            rstd = sst[:, m, 5:6]
+            a = sst[:, m, 6:7]
+            r1 = sst[:, m, 7:8]
+            nc.scalar.activation(out=rstd, in_=sst[:, m, 4:5], func=RSFUNC, bias=epscol[:, 0:1], scale=1.0 / N)
+            nc.scalar.activation(out=a, in_=negmean, func=ACT.Copy, scale=rstd)
+            nc.scalar.activation(out=lm[m][:, 0:1], in_=negmean, func=ACT.Copy, scale=rstd)
+            nc.scalar.activation(out=r1, in_=lm[m][:, 0:1], func=ACT.Identity, scale=-1.0, bias=a)
+            nc.scalar.activation(out=lm[m][:, 1:2], in_=lm[m][:, 0:1], func=ACT.Identity, scale=-1.0, bias=a)
+            nc.scalar.activation(out=lm[m][:, 2:3], in_=lm[m][:, 1:2], func=ACT.Identity, scale=-1.0, bias=r1)
 
         lt_ps = {}
         lt_sb = {}
         r_ps = {}
         o = {}
 
-        R_BANKS = ((tp, "t1"), (tp, "t2"), (tp, "t3"), (accp, "a0"), (accp, "a1"), (accp, "a2"), (accp, "a3"))
-
         def pt(m):
             if m == 0:
-                lt_ps[0] = tp.tile([P, NB, P], F32, name="t0", tag="t0")
-            nc.tensor.transpose(lt_ps[0][:, m, :], lm[m][:], ident_f[:])
+                lt_ps[0] = bank(5, [P, NB, P], BF16)
+            nc.tensor.transpose(lt_ps[0][:, m, :], lm[m][:], ident_b[:])
 
-        def sl(m, eng_copy):
-            lt_sb[m] = keep.tile([P, P], F32, name="lt_sb%d" % m)
-            eng_copy(out=lt_sb[m][:], in_=lt_ps[0][:, m, :])
+        def sl(m):
+            lt_sb[m] = keep.tile([P, P], BF16, name="lt_sb%d" % m)
+            nc.scalar.copy(out=lt_sb[m][:], in_=lt_ps[0][:, m, :])
 
-        def pr(m):
-            for c in range(3):
-                pool, tag = R_BANKS[(3 * m + c) % 7]
-                r_ps[(m, c)] = pool.tile([P, CW], F32, name=tag, tag=tag)
-                nc.tensor.matmul(out=r_ps[(m, c)][:], lhsT=lt_sb[m][:], rhs=x32[:, cols(c)], start=True, stop=True)
+        def pr(m, c):
+            r_ps[(m, c)] = bank(RB[(3 * m + c) % 3], [P, CW], F32)
+            nc.tensor.matmul(out=r_ps[(m, c)][:], lhsT=lt_sb[m][:], rhs=xrows[:, cols(c)], start=True, stop=True)
 
         def bb(m, c):
             if c == 0:
@@ -226,127 +243,117 @@ def tile_hierarchicalattention_pb_kernel(tc, ctx_heads, Wo, bo, features, ln_g, 
             nc.vector.reciprocal(out=vst[:, m, 1:2], in_=vst[:, m, 0:1])
 
         def rr(m):
-            nc.vector.tensor_scalar(out=vst[:, m, 2:3], in0=vst[:, m, 1:2], scalar1=448.0, scalar2=None, op0=ALU.mult)
+            nc.scalar.activation(out=sca[:, m:m + 1], in_=vst[:, m, 1:2], func=ACT.Copy, scale=448.0)
 
         def kk(m, split):
             o8 = work.tile([P, N], FP8, name="o8")
-            nc.scalar.activation(out=o8[:, 0:split], in_=o[m][:, 0:split], func=ACT.Identity, scale=vst[:, m, 2:3], bias=zcol[:, 0:1], saturate=False)
+            nc.scalar.activation(out=o8[:, 0:split], in_=o[m][:, 0:split], func=ACT.Identity, scale=sca[:, m:m + 1], bias=zcol[:, 0:1], saturate=False)
             if split < N:
-                nc.vector.tensor_scalar(out=o8[:, split:N], in0=o[m][:, split:N], scalar1=vst[:, m, 2:3], scalar2=None, op0=ALU.mult, saturate=False)
+                nc.vector.tensor_scalar(out=o8[:, split:N], in0=o[m][:, split:N], scalar1=sca[:, m:m + 1], scalar2=None, op0=ALU.mult, saturate=False)
             nc.sync.dma_start(out=out_1[m], in_=o8[:].bitcast(U8))
 
-        V = nc.vector
-        GP = nc.gpsimd
-        res = run_w(0, (1,))
-        for g in range(G):
-            qw(res, 0, g)
-        res = run_x(0, (1,))
-        for g in range(G):
-            qx(res, 0, g)
-        vt_ps = tp.tile([P, P], BF16, name="t%d" % (unit_no[0] % 4), tag="t%d" % (unit_no[0] % 4))
-        unit_no[0] += 1
+        rw = {}
+        rx = {}
+        vt_ps = bank(5, [P, P], BF16)
         nc.tensor.transpose(vt_ps[:], vr[:], ident_b[:])
         nc.scalar.copy(out=vt[:], in_=vt_ps[:])
-        spread(0)
-        res = run_w(1, (1,))
-        p0(V, 0, 0, CW)
-        p0(V, 1, 0, CW)
-        qw(res, 1, 0)
-        p0(V, 2, 0, CW)
-        qw(res, 1, 1)
-        p0(V, 3, 0, CW)
-        qw(res, 1, 2)
+        rw[0] = run_w(0, True)
+        for g in range(G):
+            qw(rw[0], 0, g)
+        spread()
+        rx[0] = run_x(0)
+        for g in range(G):
+            qx(rx[0], 0, g)
+        rw[1] = run_w(1)
         mm(0, 0)
-        mm(0, 1)
-        res = run_x(1, (1,))
+        p0(0, 0, 2 * CW)
         for g in range(G):
-            qx(res, 1, g)
+            qw(rw[1], 1, g)
+        rx[1] = run_x(1)
         mm(1, 0)
-        mm(1, 1)
-        for m in (0, 1):
-            p1(m, 0)
-        res = run_w(2, ())
+        p0(0, 2 * CW, N)
         for g in range(G):
-            qw(res, 2, g)
-        mm(0, 2)
+            qx(rx[1], 1, g)
+        p1(0, 0)
+        rw[2] = run_w(2)
+        p0(1, 0, 2 * CW)
+        for g in range(G):
+            qw(rw[2], 2, g)
+        rw[3] = run_w(3)
+        mm(2, 0)
+        p0(1, 2 * CW, N)
+        p0(2, 0, CW)
+        for g in range(G):
+            qw(rw[3], 3, g)
+        rw[4] = run_w(4)
+        mm(3, 0)
+        p0(2, CW, N)
+        for g in range(G):
+            qw(rw[4], 4, g)
+        p1(0, 1)
+        rw[5] = run_w(5)
+        mm(4, 0)
+        for q in range(4):
+            mm(q, 1)
+        p0(3, 0, CW)
+        for g in range(G):
+            qw(rw[5], 5, g)
+        mm(5, 0)
+        p1(1, 0)
+        p1(0, 2)
+        st1(0)
+        st2(0)
+        for c in range(3):
+            p2(0, c)
+        mm(4, 1)
+        mm(5, 1)
+        p1(1, 1)
+        p0(3, CW, N)
+        p1(1, 2)
+        st1(1)
+        for c in range(3):
+            p2(1, c)
+        for q in range(6):
+            mm(q, 2)
         mm(0, 3)
-        res = run_w(3, ())
-        for g in range(G):
-            qw(res, 3, g)
-        mm(1, 2)
         mm(1, 3)
-        for m in (2, 3):
-            p1(m, 0)
-        p0(V, 0, CW, N)
-        res = run_w(4, ())
-        for g in range(G):
-            qw(res, 4, g)
-        p0(V, 1, CW, N)
-        res = run_w(5, ())
-        for g in range(G):
-            qw(res, 5, g)
-        nc.scalar.copy(out=x32[:], in_=xrows[:])
-        for m in (2, 3):
-            p0(GP, m, CW, 2 * CW)
-            p0(GP, m, 2 * CW, N)
-
-        def p2all(m):
-            for c in (0, 1, 2):
-                p2(m, c * CW, (c + 1) * CW)
-
-        def pr1(m, c):
-            pool, tag = R_BANKS[(3 * m + c) % 7]
-            r_ps[(m, c)] = pool.tile([P, CW], F32, name=tag, tag=tag)
-            nc.tensor.matmul(out=r_ps[(m, c)][:], lhsT=lt_sb[m][:], rhs=x32[:, cols(c)], start=True, stop=True)
-
-        for m in (0, 1):
-            mm(2, m)
-            mm(3, m)
-            p1(m, 1)
-            mm(4, m)
-        for m in (0, 1):
-            mm(5, m)
-            p1(m, 2)
-            stats(m)
-            p2all(m)
-        for m in (2, 3):
-            mm(2, m)
-            mm(3, m)
-            p1(m, 1)
-            mm(4, m)
-            mm(5, m)
-            if m == 3:
-                pt(0)
-                sl(0, nc.vector.tensor_copy)
-            p1(m, 2)
-        pr1(0, 0)
-        pr1(0, 1)
+        pt(0)
+        sl(0)
+        st2(1)
+        for c in range(3):
+            p1(2, c)
+        st1(2)
+        for c in range(3):
+            p2(2, c)
+        for q in range(2, 6):
+            mm(q, 3)
+        for c in range(3):
+            p1(3, c)
+        for c in range(3):
+            pr(0, c)
         pt(1)
-        sl(1, nc.scalar.copy)
-        pr1(0, 2)
-        stats(2)
-        p2all(2)
-        pr1(1, 0)
-        pr1(1, 1)
-        pt(2)
-        sl(2, nc.scalar.copy)
-        pr1(1, 2)
-        stats(3)
-        p2all(3)
+        sl(1)
+        st2(2)
+        st1(3)
+        for c in range(3):
+            p2(3, c)
         for c in range(3):
             bb(0, c)
-        pr1(2, 0)
-        pr1(2, 1)
-        pt(3)
-        sl(3, nc.scalar.copy)
-        pr1(2, 2)
-        ca(0)
+        for c in range(3):
+            pr(1, c)
+        pt(2)
+        sl(2)
+        st2(3)
         bb(1, 0)
-        rc(0)
+        ca(0)
         bb(1, 1)
-        rr(0)
+        rc(0)
         bb(1, 2)
-        pr(3)
+        for c in range(3):
+            pr(2, c)
+        pt(3)
+        sl(3)
+        rr(0)
         kk(0, N)
         bb(2, 0)
         ca(1)
@@ -355,6 +362,8 @@ def tile_hierarchicalattention_pb_kernel(tc, ctx_heads, Wo, bo, features, ln_g, 
         bb(2, 2)
         rr(1)
         kk(1, N)
+        for c in range(3):
+            pr(3, c)
         bb(3, 0)
         ca(2)
         bb(3, 1)

@@ -30,7 +30,7 @@ def tile_hierarchicalattention_pb_kernel(tc, ctx_heads, Wo, bo, features, ln_g, 
     nc = tc.nc
     with ExitStack() as es:
         keep = es.enter_context(tc.tile_pool(name="keep", bufs=1))
-        gp = es.enter_context(tc.tile_pool(name="gp", bufs=6))
+        gp = es.enter_context(tc.tile_pool(name="gp", bufs=3))
         work = es.enter_context(tc.tile_pool(name="work", bufs=2))
         op = es.enter_context(tc.tile_pool(name="op", bufs=4))
         ps = es.enter_context(tc.psum_pool(name="ps", bufs=1))
@@ -103,10 +103,10 @@ def tile_hierarchicalattention_pb_kernel(tc, ctx_heads, Wo, bo, features, ln_g, 
         wo_words = [wo_raw[r // 2][:, r % 2, :].bitcast(F32) for r in range(12)]
         ctx_words = [ctx_raw[b // 2][:, b % 2, :].bitcast(F32) for b in range(NB)]
 
-        wo_codes = keep.tile([P, G, N], U32, name="wo_codes", align_bytes=64)
-        wo_scales = keep.tile([P, G, N], U8, name="wo_scales", align_bytes=64)
-        cx_codes = keep.tile([P, G, 512], U32, name="cx_codes", align_bytes=64)
-        cx_scales = keep.tile([P, G, 512], U8, name="cx_scales", align_bytes=64)
+        wo_codes = keep.tile([P, 6 * G * QW], U32, name="wo_codes", align_bytes=64)
+        wo_scales = keep.tile([P, 6 * G * QW], U8, name="wo_scales", align_bytes=64)
+        cx_codes = keep.tile([P, 2 * G * QW], U32, name="cx_codes", align_bytes=64)
+        cx_scales = keep.tile([P, 2 * G * QW], U8, name="cx_scales", align_bytes=64)
 
         vt = keep.tile([P, P], BF16, name="vt")
         fb = [keep.tile([P, N], F32, name="fb%d" % m) for m in range(NB)]
@@ -146,12 +146,10 @@ def tile_hierarchicalattention_pb_kernel(tc, ctx_heads, Wo, bo, features, ln_g, 
                     for g in range(G):
                         for u in range(2):
                             nc.tensor.transpose(xts[g][:, i, u, :], words2[i][:, 256 * g + u:256 * (g + 1):2], ident_f[:])
-            res = []
+            grouped = gp.tile([P, G * 1024], BF16, name="grouped", align_bytes=64)
             for g in range(G):
-                grouped = gp.tile([P, 1024], BF16, name="grouped", align_bytes=64)
-                nc.scalar.copy(out=grouped[:].bitcast(F32).rearrange("p (i n u) -> p i n u", i=2, u=2), in_=xts[g][:].rearrange("p i u n -> p i n u"))
-                res.append(grouped)
-            return res
+                nc.scalar.copy(out=grouped[:, g * 1024:(g + 1) * 1024].bitcast(F32).rearrange("p (i n u) -> p i n u", i=2, u=2), in_=xts[g][:].rearrange("p i u n -> p i n u"))
+            return grouped
 
         def run_w(q, by_tile=False):
             return run_t((wo_words[2 * q], wo_words[2 * q + 1]), by_tile)
@@ -159,11 +157,18 @@ def tile_hierarchicalattention_pb_kernel(tc, ctx_heads, Wo, bo, features, ln_g, 
         def run_x(q):
             return run_t((ctx_words[2 * q], ctx_words[2 * q + 1]))
 
-        def qw(res, q, g):
-            nc.vector.quantize_mx(out=wo_codes[:, g, QW * q:QW * (q + 1)].bitcast(FP8X4), scales=wo_scales[:, g, QW * q:QW * (q + 1)], in_=res[g][:])
+        def quant(codes, scales, grouped, q, g0, g1):
+            lo = (q * G + g0) * QW
+            hi = (q * G + g1) * QW
+            nc.vector.quantize_mx(out=codes[:, lo:hi].bitcast(FP8X4), scales=scales[:, lo:hi], in_=grouped[:, g0 * 1024:g1 * 1024])
 
-        def qx(res, q, g):
-            nc.vector.quantize_mx(out=cx_codes[:, g, QW * q:QW * (q + 1)].bitcast(FP8X4), scales=cx_scales[:, g, QW * q:QW * (q + 1)], in_=res[g][:])
+        def qw(grouped, q):
+            quant(wo_codes, wo_scales, grouped, q, 0, 2)
+            quant(wo_codes, wo_scales, grouped, q, 2, 3)
+
+        def qx(grouped, q):
+            quant(cx_codes, cx_scales, grouped, q, 0, 2)
+            quant(cx_codes, cx_scales, grouped, q, 2, 3)
 
         acc = {}
         ABANK = {(0, 0): 5, (0, 1): 6, (0, 2): 7, (1, 0): 4, (1, 1): 0, (1, 2): 1, (2, 0): 2, (2, 1): 4, (2, 2): 0, (3, 0): 1, (3, 1): 2, (3, 2): 4}
@@ -172,15 +177,16 @@ def tile_hierarchicalattention_pb_kernel(tc, ctx_heads, Wo, bo, features, ln_g, 
         def mm(q, m):
             c = q // 2
             h = q % 2
+            xo = (m // 2) * G * QW + (m % 2) * P
             if h == 0:
                 acc[(m, c)] = bank(ABANK[(m, c)], [P, CW], F32)
             for g in range(G):
                 nc.tensor.matmul_mx(
                     out=acc[(m, c)][:, h * QW:(h + 1) * QW],
-                    lhsT=cx_codes[:, g, P * m:P * (m + 1)].bitcast(FP8X4),
-                    lhsT_scale=cx_scales[:, g, P * m:P * (m + 1)],
-                    rhs=wo_codes[:, g, QW * q:QW * (q + 1)].bitcast(FP8X4),
-                    rhs_scale=wo_scales[:, g, QW * q:QW * (q + 1)],
+                    lhsT=cx_codes[:, xo + g * QW:xo + g * QW + P].bitcast(FP8X4),
+                    lhsT_scale=cx_scales[:, xo + g * QW:xo + g * QW + P],
+                    rhs=wo_codes[:, (q * G + g) * QW:(q * G + g + 1) * QW].bitcast(FP8X4),
+                    rhs_scale=wo_scales[:, (q * G + g) * QW:(q * G + g + 1) * QW],
                     start=(g == 0),
                     stop=(g == G - 1),
                 )
@@ -258,55 +264,47 @@ def tile_hierarchicalattention_pb_kernel(tc, ctx_heads, Wo, bo, features, ln_g, 
         nc.tensor.transpose(vt_ps[:], vr[:], ident_b[:])
         nc.scalar.copy(out=vt[:], in_=vt_ps[:])
         rw[0] = run_w(0, True)
-        for g in range(G):
-            qw(rw[0], 0, g)
+        qw(rw[0], 0)
         spread()
         rx[0] = run_x(0)
-        for g in range(G):
-            qx(rx[0], 0, g)
+        qx(rx[0], 0)
         rw[1] = run_w(1)
         mm(0, 0)
         p0(0, 0, 2 * CW)
-        for g in range(G):
-            qw(rw[1], 1, g)
+        qw(rw[1], 1)
         rx[1] = run_x(1)
         mm(1, 0)
         p0(0, 2 * CW, N)
-        for g in range(G):
-            qx(rx[1], 1, g)
+        qx(rx[1], 1)
         p1(0, 0)
         rw[2] = run_w(2)
         p0(1, 0, 2 * CW)
-        for g in range(G):
-            qw(rw[2], 2, g)
+        qw(rw[2], 2)
         rw[3] = run_w(3)
         mm(2, 0)
         p0(1, 2 * CW, N)
         p0(2, 0, CW)
-        for g in range(G):
-            qw(rw[3], 3, g)
+        qw(rw[3], 3)
         rw[4] = run_w(4)
         mm(3, 0)
         p0(2, CW, N)
-        for g in range(G):
-            qw(rw[4], 4, g)
+        qw(rw[4], 4)
         p1(0, 1)
         rw[5] = run_w(5)
         mm(4, 0)
-        for q in range(4):
+        for q in range(2):
             mm(q, 1)
         p0(3, 0, CW)
-        for g in range(G):
-            qw(rw[5], 5, g)
+        qw(rw[5], 5)
         mm(5, 0)
         p1(1, 0)
         p1(0, 2)
         st1(0)
         st2(0)
-        for c in range(3):
+        for c in (2, 0, 1):
             p2(0, c)
-        mm(4, 1)
-        mm(5, 1)
+        for q in range(2, 6):
+            mm(q, 1)
         p1(1, 1)
         p0(3, CW, N)
         p1(1, 2)

@@ -87,17 +87,17 @@ def tile_hierarchicalattention_pb_kernel(tc, ctx_heads, Wo, bo, features, ln_g, 
         load_x(0)
         load_f(0)
         load_w(1)
-        load_x(1)
-        load_w(2)
         load_f(1)
+        load_w(2)
+        load_f(2)
+        load_w(3)
+        load_f(3)
+        load_w(4)
+        load_w(5)
+        load_x(1)
         for r in range(3):
             nc.sync.dma_start(out=xrows[r:r + 1, :], in_=ln_g.rearrange("(o n) -> o n", o=1))
         nc.sync.dma_start(out=xrows[4:5, :], in_=ln_b.rearrange("(o n) -> o n", o=1))
-        load_w(3)
-        load_f(2)
-        load_w(4)
-        load_w(5)
-        load_f(3)
         nc.sync.dma_start(out=g_b, in_=ln_g.partition_broadcast(P))
 
         wo_words = [wo_raw[r // 2][:, r % 2, :].bitcast(F32) for r in range(12)]
@@ -131,12 +131,12 @@ def tile_hierarchicalattention_pb_kernel(tc, ctx_heads, Wo, bo, features, ln_g, 
         TB = (0, 1, 2, 3, 4)
         unit_no = [0]
 
-        def run_t(words2, by_tile=False):
-            xts = []
-            for g in range(G):
+        def run_t(words2, by_tile=False, gs=(0, 1, 2), grouped=None):
+            xts = {}
+            for g in gs:
                 xt = bank(TB[unit_no[0] % len(TB)], [P, 2, 2, P], F32)
                 unit_no[0] += 1
-                xts.append(xt)
+                xts[g] = xt
                 if not by_tile:
                     for i in range(2):
                         for u in range(2):
@@ -146,16 +146,17 @@ def tile_hierarchicalattention_pb_kernel(tc, ctx_heads, Wo, bo, features, ln_g, 
                     for g in range(G):
                         for u in range(2):
                             nc.tensor.transpose(xts[g][:, i, u, :], words2[i][:, 256 * g + u:256 * (g + 1):2], ident_f[:])
-            grouped = gp.tile([P, G * 1024], BF16, name="grouped", align_bytes=64)
-            for g in range(G):
+            if grouped is None:
+                grouped = gp.tile([P, G * 1024], BF16, name="grouped", align_bytes=64)
+            for g in gs:
                 nc.scalar.copy(out=grouped[:, g * 1024:(g + 1) * 1024].bitcast(F32).rearrange("p (i n u) -> p i n u", i=2, u=2), in_=xts[g][:].rearrange("p i u n -> p i n u"))
             return grouped
 
         def run_w(q, by_tile=False):
             return run_t((wo_words[2 * q], wo_words[2 * q + 1]), by_tile)
 
-        def run_x(q):
-            return run_t((ctx_words[2 * q], ctx_words[2 * q + 1]))
+        def run_x(q, gs=(0, 1, 2), grouped=None):
+            return run_t((ctx_words[2 * q], ctx_words[2 * q + 1]), False, gs, grouped)
 
         def quant(codes, scales, grouped, q, g0, g1):
             lo = (q * G + g0) * QW
@@ -267,50 +268,48 @@ def tile_hierarchicalattention_pb_kernel(tc, ctx_heads, Wo, bo, features, ln_g, 
         qw(rw[0], 0)
         spread()
         rx[0] = run_x(0)
+        p0(0, 0, CW)
         qx(rx[0], 0)
         rw[1] = run_w(1)
         mm(0, 0)
-        p0(0, 0, 2 * CW)
+        p0(0, CW, N)
+        p0(1, 0, CW)
         qw(rw[1], 1)
-        rx[1] = run_x(1)
-        mm(1, 0)
-        p0(0, 2 * CW, N)
-        qx(rx[1], 1)
-        p1(0, 0)
         rw[2] = run_w(2)
-        p0(1, 0, 2 * CW)
+        mm(1, 0)
+        p0(1, CW, N)
         qw(rw[2], 2)
+        p1(0, 0)
         rw[3] = run_w(3)
         mm(2, 0)
-        p0(1, 2 * CW, N)
-        p0(2, 0, CW)
+        p0(2, 0, N)
         qw(rw[3], 3)
         rw[4] = run_w(4)
         mm(3, 0)
-        p0(2, CW, N)
+        p0(3, 0, 2 * CW)
         qw(rw[4], 4)
         p1(0, 1)
         rw[5] = run_w(5)
         mm(4, 0)
-        for q in range(2):
-            mm(q, 1)
-        p0(3, 0, CW)
+        p0(3, 2 * CW, N)
         qw(rw[5], 5)
+        rx[1] = run_x(1, (0, 1))
         mm(5, 0)
-        p1(1, 0)
+        run_x(1, (2,), rx[1])
         p1(0, 2)
         st1(0)
         st2(0)
+        qx(rx[1], 1)
+        for q in range(6):
+            mm(q, 1)
+        for c in range(3):
+            p1(1, c)
+        p2(1, 0)
         for c in (2, 0, 1):
             p2(0, c)
-        for q in range(2, 6):
-            mm(q, 1)
-        p1(1, 1)
-        p0(3, CW, N)
-        p1(1, 2)
+        p2(1, 1)
+        p2(1, 2)
         st1(1)
-        for c in range(3):
-            p2(1, c)
         for q in range(6):
             mm(q, 2)
         mm(0, 3)

@@ -128,7 +128,7 @@ def tile_hierarchicalattention_pb_kernel(tc, ctx_heads, Wo, bo, features, ln_g, 
                     nc.tensor.transpose(pst[:, j * P:(j + 1) * P], vt[:, i:i + 1].to_broadcast([P, P]), ident_b[:])
                 nc.vector.tensor_copy(out=vec_b[:, first * P:(first + count) * P], in_=pst[:, 0:count * P])
 
-        TB = (0, 1, 2, 3, 4)
+        TB = (0, 1, 2, 3)
         unit_no = [0]
 
         def run_t(words2, by_tile=False, gs=(0, 1, 2), grouped=None):
@@ -172,8 +172,8 @@ def tile_hierarchicalattention_pb_kernel(tc, ctx_heads, Wo, bo, features, ln_g, 
             quant(cx_codes, cx_scales, grouped, q, 2, 3)
 
         acc = {}
-        ABANK = {(0, 0): 5, (0, 1): 6, (0, 2): 7, (1, 0): 4, (1, 1): 0, (1, 2): 1, (2, 0): 2, (2, 1): 4, (2, 2): 0, (3, 0): 1, (3, 1): 2, (3, 2): 4}
-        RB = (6, 7, 3)
+        ABANK = {(0, 0): 5, (0, 1): 6, (0, 2): 5, (1, 0): 7, (1, 1): 4, (1, 2): 6, (2, 0): 0, (2, 1): 1, (2, 2): 2, (3, 0): 3, (3, 1): 0, (3, 2): 1}
+        RB = (7, 4, 6)
 
         def mm(q, m):
             c = q // 2
@@ -272,20 +272,24 @@ def tile_hierarchicalattention_pb_kernel(tc, ctx_heads, Wo, bo, features, ln_g, 
         qx(rx[0], 0)
         rw[1] = run_w(1)
         mm(0, 0)
+        mm(0, 1)
         p0(0, CW, N)
         p0(1, 0, CW)
         qw(rw[1], 1)
         rw[2] = run_w(2)
         mm(1, 0)
+        mm(1, 1)
         p0(1, CW, N)
         qw(rw[2], 2)
         p1(0, 0)
         rw[3] = run_w(3)
         mm(2, 0)
+        mm(2, 1)
         p0(2, 0, N)
         qw(rw[3], 3)
         rw[4] = run_w(4)
         mm(3, 0)
+        mm(3, 1)
         p0(3, 0, 2 * CW)
         qw(rw[4], 4)
         p1(0, 1)
@@ -299,15 +303,16 @@ def tile_hierarchicalattention_pb_kernel(tc, ctx_heads, Wo, bo, features, ln_g, 
         p1(0, 2)
         st1(0)
         st2(0)
+        p1(1, 0)
         qx(rx[1], 1)
-        for q in range(6):
-            mm(q, 1)
-        for c in range(3):
-            p1(1, c)
-        p2(1, 0)
+        mm(4, 1)
+        mm(5, 1)
+        p1(1, 1)
+        p1(1, 2)
+        p2(1, 1)
         for c in (2, 0, 1):
             p2(0, c)
-        p2(1, 1)
+        p2(1, 0)
         p2(1, 2)
         st1(1)
         for q in range(6):

@@ -231,7 +231,7 @@ def tile_hierarchicalattention_pb_kernel(tc, ctx_heads, Wo, bo, features, ln_g, 
 
         def sl(m):
             lt_sb[m] = keep.tile([P, P], BF16, name="lt_sb%d" % m)
-            nc.scalar.copy(out=lt_sb[m][:], in_=lt_ps[0][:, m, :])
+            nc.vector.tensor_copy(out=lt_sb[m][:], in_=lt_ps[0][:, m, :])
 
         def pr(m, c):
             r_ps[(m, c)] = bank(RB[(3 * m + c) % 3], [P, CW], F32)
@@ -315,50 +315,51 @@ def tile_hierarchicalattention_pb_kernel(tc, ctx_heads, Wo, bo, features, ln_g, 
         p2(1, 0)
         p2(1, 2)
         st1(1)
+        st2(1)
         for q in range(6):
             mm(q, 2)
         mm(0, 3)
         mm(1, 3)
         pt(0)
-        sl(0)
-        st2(1)
         for c in range(3):
             p1(2, c)
         st1(2)
+        st2(2)
         for c in range(3):
             p2(2, c)
+        sl(0)
         for q in range(2, 6):
             mm(q, 3)
         for c in range(3):
             p1(3, c)
-        for c in range(3):
-            pr(0, c)
-        pt(1)
-        sl(1)
-        st2(2)
         st1(3)
+        st2(3)
         for c in range(3):
             p2(3, c)
         for c in range(3):
-            bb(0, c)
+            pr(0, c)
+        pt(1)
+        bb(0, 0)
+        bb(0, 1)
+        sl(1)
+        bb(0, 2)
         for c in range(3):
             pr(1, c)
         pt(2)
-        sl(2)
-        st2(3)
         bb(1, 0)
         ca(0)
+        sl(2)
         bb(1, 1)
         rc(0)
         bb(1, 2)
         for c in range(3):
             pr(2, c)
         pt(3)
-        sl(3)
         rr(0)
         kk(0, N)
         bb(2, 0)
         ca(1)
+        sl(3)
         bb(2, 1)
         rc(1)
         bb(2, 2)

@@ -252,11 +252,14 @@ def tile_hierarchicalattention_pb_kernel(tc, ctx_heads, Wo, bo, features, ln_g, 
         def rr(m):
             nc.scalar.activation(out=sca[:, m:m + 1], in_=vst[:, m, 1:2], func=ACT.Copy, scale=448.0)
 
+        def rrv(m):
+            nc.vector.tensor_scalar(out=sca[:, m:m + 1], in0=vst[:, m, 1:2], scalar1=448.0, scalar2=None, op0=ALU.mult)
+
         def kk(m, split):
             o8 = work.tile([P, N], FP8, name="o8")
-            nc.scalar.activation(out=o8[:, 0:split], in_=o[m][:, 0:split], func=ACT.Identity, scale=sca[:, m:m + 1], bias=zcol[:, 0:1], saturate=False)
             if split < N:
                 nc.vector.tensor_scalar(out=o8[:, split:N], in0=o[m][:, split:N], scalar1=sca[:, m:m + 1], scalar2=None, op0=ALU.mult, saturate=False)
+            nc.scalar.activation(out=o8[:, 0:split], in_=o[m][:, 0:split], func=ACT.Identity, scale=sca[:, m:m + 1], bias=zcol[:, 0:1], saturate=False)
             nc.sync.dma_start(out=out_1[m], in_=o8[:].bitcast(U8))
 
         rw = {}
@@ -376,5 +379,5 @@ def tile_hierarchicalattention_pb_kernel(tc, ctx_heads, Wo, bo, features, ln_g, 
         kk(2, N)
         ca(3)
         rc(3)
-        rr(3)
+        rrv(3)
         kk(3, CW)

@@ -42,14 +42,14 @@ def tile_hierarchicalattention_pb_kernel(tc, ctx_heads, Wo, bo, features, ln_g, 
 
         vr = keep.tile([P, P], BF16, name="vr")
         nc.gpsimd.memset(vr[:], 0.0)
-        xrows = keep.tile([P, N], BF16, name="xrows")
-        nc.vector.memset(xrows[:], 0.0)
         onecol = keep.tile([P, 1], F32, name="onecol")
         nc.vector.memset(onecol[:], 1.0)
         zcol = keep.tile([P, 1], F32, name="zcol")
         nc.vector.memset(zcol[:], 0.0)
         epscol = keep.tile([P, 1], F32, name="epscol")
         nc.vector.memset(epscol[:], EPS)
+        xrows = keep.tile([P, N], BF16, name="xrows")
+        nc.vector.memset(xrows[:], 0.0)
         warm = keep.tile([P, 1], F32, name="warm")
         nc.scalar.activation(out=warm[:], in_=onecol[:], func=RSFUNC)
 
@@ -128,6 +128,11 @@ def tile_hierarchicalattention_pb_kernel(tc, ctx_heads, Wo, bo, features, ln_g, 
                     nc.tensor.transpose(pst[:, j * P:(j + 1) * P], vt[:, i:i + 1].to_broadcast([P, P]), ident_b[:])
                 nc.vector.tensor_copy(out=vec_b[:, first * P:(first + count) * P], in_=pst[:, 0:count * P])
 
+        def turn_bo():
+            vt_ps = bank(5, [P, P], BF16)
+            nc.tensor.transpose(vt_ps[:], vr[:], ident_b[:])
+            nc.scalar.copy(out=vt[:], in_=vt_ps[:])
+
         TB = (0, 1, 2, 3)
         unit_no = [0]
 
@@ -143,6 +148,8 @@ def tile_hierarchicalattention_pb_kernel(tc, ctx_heads, Wo, bo, features, ln_g, 
                             nc.tensor.transpose(xt[:, i, u, :], words2[i][:, 256 * g + u:256 * (g + 1):2], ident_f[:])
             if by_tile:
                 for i in range(2):
+                    if i == 1:
+                        turn_bo()
                     for g in range(G):
                         for u in range(2):
                             nc.tensor.transpose(xts[g][:, i, u, :], words2[i][:, 256 * g + u:256 * (g + 1):2], ident_f[:])
@@ -264,9 +271,6 @@ def tile_hierarchicalattention_pb_kernel(tc, ctx_heads, Wo, bo, features, ln_g, 
 
         rw = {}
         rx = {}
-        vt_ps = bank(5, [P, P], BF16)
-        nc.tensor.transpose(vt_ps[:], vr[:], ident_b[:])
-        nc.scalar.copy(out=vt[:], in_=vt_ps[:])
         rw[0] = run_w(0, True)
         qw(rw[0], 0)
         spread()

from contextlib import ExitStack

import concourse.masks as masks
import concourse.mybir as mybir

F32 = mybir.dt.float32
BF16 = mybir.dt.bfloat16
U32 = mybir.dt.uint32
U8 = mybir.dt.uint8
FP8X4 = mybir.dt.float8_e4m3fn_x4
FP8 = mybir.dt.float8_e4m3fn
ALU = mybir.AluOpType
ACT = mybir.ActivationFunctionType
AX = mybir.AxisListType
RSFUNC = ACT.Abs_reciprocal_sqrt

P = 128
NB = 4
K = 1536
N = 1536
G = 3
CW = 512
QW = 256
EPS = 1e-5

FLOPS = 2 * 512 * 1536 * 1536


def tile_hierarchicalattention_pb_kernel(tc, ctx_heads, Wo, bo, features, ln_g, ln_b, out_0, out_1):
    nc = tc.nc
    with ExitStack() as es:
        keep = es.enter_context(tc.tile_pool(name="keep", bufs=1))
        gp = es.enter_context(tc.tile_pool(name="gp", bufs=3))
        work = es.enter_context(tc.tile_pool(name="work", bufs=2))
        op = es.enter_context(tc.tile_pool(name="op", bufs=4))
        ps = es.enter_context(tc.psum_pool(name="ps", bufs=1))
        es.enter_context(tc.manual_schedule())

        def bank(i, shape, dtype):
            t = ps.tile(shape, dtype, name="b%d" % i, tag="b%d" % i)
            return t

        vr = keep.tile([P, P], BF16, name="vr")
        nc.gpsimd.memset(vr[:], 0.0)
        onecol = keep.tile([P, 1], F32, name="onecol")
        nc.vector.memset(onecol[:], 1.0)
        zcol = keep.tile([P, 1], F32, name="zcol")
        nc.vector.memset(zcol[:], 0.0)
        epscol = keep.tile([P, 1], F32, name="epscol")
        nc.vector.memset(epscol[:], EPS)
        xrows = keep.tile([P, N], BF16, name="xrows")
        nc.vector.memset(xrows[:], 0.0)
        warm = keep.tile([P, 1], F32, name="warm")
        nc.scalar.activation(out=warm[:], in_=onecol[:], func=RSFUNC)

        ident_f = keep.tile([P, P], F32, name="ident_f")
        masks.make_identity(nc, ident_f[:])
        ident_b = keep.tile([P, P], BF16, name="ident_b")
        masks.make_identity(nc, ident_b[:])
        lm = [keep.tile([P, P], BF16, name="lm%d" % m) for m in range(NB)]
        for m in range(NB):
            nc.gpsimd.memset(lm[m][:], 0.0)
            nc.gpsimd.memset(lm[m][:, 4:5], 1.0)

        wo_raw = [keep.tile([P, 2, K], BF16, name="wo_raw%d" % q) for q in range(6)]
        ctx_raw = [keep.tile([P, 2, K], BF16, name="ctx_raw%d" % q) for q in range(2)]
        f = [keep.tile([P, N], BF16, name="f%d" % m) for m in range(NB)]
        vec_b = keep.tile([P, 2 * N], BF16, name="vec_b")
        bo_b = vec_b[:, 0:N]
        g_b = vec_b[:, N:2 * N]

        def load_w(q):
            nc.sync.dma_start(out=wo_raw[q][:], in_=Wo[2 * P * q:2 * P * (q + 1), :].rearrange("(i p) k -> p i k", i=2))

        def load_w_half(q, i):
            nc.sync.dma_start(out=wo_raw[q][:, i, :], in_=Wo[P * (2 * q + i):P * (2 * q + i + 1), :])

        def load_x(q):
            nc.sync.dma_start(out=ctx_raw[q][:].rearrange("p i (h d) -> p (i h) d", d=128), in_=ctx_heads[2 * q:2 * q + 2].rearrange("b h s d -> s (b h) d"))

        def load_f(m):
            nc.sync.dma_start(out=f[m][:], in_=features[m])

        load_w_half(0, 0)
        nc.sync.dma_start(out=vr[0:12, :], in_=bo.rearrange("(c j) -> c j", c=12))
        load_w_half(0, 1)
        load_x(0)
        load_f(0)
        load_w(1)
        load_f(1)
        load_w(2)
        load_f(2)
        load_w(3)
        load_f(3)
        load_w(4)
        load_w(5)
        load_x(1)
        for r in range(3):
            nc.sync.dma_start(out=xrows[r:r + 1, :], in_=ln_g.rearrange("(o n) -> o n", o=1))
        nc.sync.dma_start(out=xrows[4:5, :], in_=ln_b.rearrange("(o n) -> o n", o=1))
        nc.sync.dma_start(out=g_b, in_=ln_g.partition_broadcast(P))

        wo_words = [wo_raw[r // 2][:, r % 2, :].bitcast(F32) for r in range(12)]
        ctx_words = [ctx_raw[b // 2][:, b % 2, :].bitcast(F32) for b in range(NB)]

        wo_codes = keep.tile([P, 6 * G * QW], U32, name="wo_codes", align_bytes=64)
        wo_scales = keep.tile([P, 6 * G * QW], U8, name="wo_scales", align_bytes=64)
        cx_codes = keep.tile([P, 2 * G * QW], U32, name="cx_codes", align_bytes=64)
        cx_scales = keep.tile([P, 2 * G * QW], U8, name="cx_scales", align_bytes=64)

        vt = keep.tile([P, P], BF16, name="vt")
        fb = [keep.tile([P, N], F32, name="fb%d" % m) for m in range(NB)]
        y = [keep.tile([P, N], F32, name="y%d" % m) for m in range(NB)]
        yg = [keep.tile([P, N], F32, name="yg%d" % m) for m in range(NB)]
        sums = keep.tile([P, NB, 4], F32, name="sums")
        sst = keep.tile([P, NB, 8], F32, name="sst")
        vst = keep.tile([P, NB, 4], F32, name="vst")
        sca = keep.tile([P, NB], F32, name="sca")

        def cols(c):
            return slice(c * CW, (c + 1) * CW)

        def spread():
            for first, count, b in ((0, 8, 6), (8, 4, 7)):
                pst = bank(b, [P, 1024], BF16)
                for j in range(count):
                    i = first + j
                    nc.tensor.transpose(pst[:, j * P:(j + 1) * P], vt[:, i:i + 1].to_broadcast([P, P]), ident_b[:])
                nc.vector.tensor_copy(out=vec_b[:, first * P:(first + count) * P], in_=pst[:, 0:count * P])

        def turn_bo():
            vt_ps = bank(5, [P, P], BF16)
            nc.tensor.transpose(vt_ps[:], vr[:], ident_b[:])
            nc.scalar.copy(out=vt[:], in_=vt_ps[:])

        TB = (0, 1, 2, 3)
        unit_no = [0]

        def run_t(words2, by_tile=False, gs=(0, 1, 2), grouped=None):
            xts = {}
            for g in gs:
                xt = bank(TB[unit_no[0] % len(TB)], [P, 2, 2, P], F32)
                unit_no[0] += 1
                xts[g] = xt
                if not by_tile:
                    for i in range(2):
                        for u in range(2):
                            nc.tensor.transpose(xt[:, i, u, :], words2[i][:, 256 * g + u:256 * (g + 1):2], ident_f[:])
            if by_tile:
                for i in range(2):
                    if i == 1:
                        turn_bo()
                    for g in range(G):
                        for u in range(2):
                            nc.tensor.transpose(xts[g][:, i, u, :], words2[i][:, 256 * g + u:256 * (g + 1):2], ident_f[:])
            if grouped is None:
                grouped = gp.tile([P, G * 1024], BF16, name="grouped", align_bytes=64)
            for g in gs:
                nc.scalar.copy(out=grouped[:, g * 1024:(g + 1) * 1024].bitcast(F32).rearrange("p (i n u) -> p i n u", i=2, u=2), in_=xts[g][:].rearrange("p i u n -> p i n u"))
            return grouped

        def run_w(q, by_tile=False):
            return run_t((wo_words[2 * q], wo_words[2 * q + 1]), by_tile)

        def run_x(q, gs=(0, 1, 2), grouped=None):
            return run_t((ctx_words[2 * q], ctx_words[2 * q + 1]), False, gs, grouped)

        def quant(codes, scales, grouped, q, g0, g1):
            lo = (q * G + g0) * QW
            hi = (q * G + g1) * QW
            nc.vector.quantize_mx(out=codes[:, lo:hi].bitcast(FP8X4), scales=scales[:, lo:hi], in_=grouped[:, g0 * 1024:g1 * 1024])

        def qw(grouped, q):
            quant(wo_codes, wo_scales, grouped, q, 0, 2)
            quant(wo_codes, wo_scales, grouped, q, 2, 3)

        def qx(grouped, q):
            quant(cx_codes, cx_scales, grouped, q, 0, 2)
            quant(cx_codes, cx_scales, grouped, q, 2, 3)

        acc = {}
        ABANK = {(0, 0): 5, (0, 1): 6, (0, 2): 5, (1, 0): 7, (1, 1): 4, (1, 2): 6, (2, 0): 0, (2, 1): 1, (2, 2): 2, (3, 0): 3, (3, 1): 0, (3, 2): 1}
        RB = (7, 4, 6)

        def mm(q, m):
            c = q // 2
            h = q % 2
            xo = (m // 2) * G * QW + (m % 2) * P
            if h == 0:
                acc[(m, c)] = bank(ABANK[(m, c)], [P, CW], F32)
            for g in range(G):
                nc.tensor.matmul_mx(
                    out=acc[(m, c)][:, h * QW:(h + 1) * QW],
                    lhsT=cx_codes[:, xo + g * QW:xo + g * QW + P].bitcast(FP8X4),
                    lhsT_scale=cx_scales[:, xo + g * QW:xo + g * QW + P],
                    rhs=wo_codes[:, (q * G + g) * QW:(q * G + g + 1) * QW].bitcast(FP8X4),
                    rhs_scale=wo_scales[:, (q * G + g) * QW:(q * G + g + 1) * QW],
                    start=(g == 0),
                    stop=(g == G - 1),
                )

        def p0(m, lo, hi):
            nc.vector.tensor_tensor(out=fb[m][:, lo:hi], in0=f[m][:, lo:hi], in1=bo_b[:, lo:hi], op=ALU.add)

        def p1(m, c):
            nc.vector.scalar_tensor_tensor(out=y[m][:, cols(c)], in0=acc[(m, c)][:], scalar=1.0, in1=fb[m][:, cols(c)], op0=ALU.mult, op1=ALU.add, accum_out=sums[:, m, c:c + 1])

        def p2(m, c):
            nc.gpsimd.tensor_tensor(out=yg[m][:, cols(c)], in0=y[m][:, cols(c)], in1=g_b[:, cols(c)], op=ALU.mult)

        def st1(m):
            negmean = sst[:, m, 3:4]
            nc.scalar.activation(out=sst[:, m, 0:3], in_=sums[:, m, 0:3], func=ACT.Copy, scale=-1.0 / N, accum_out=negmean)
            junk = work.tile([P, N], BF16, name="junk")
            nc.scalar.activation(out=junk[:], in_=y[m][:], func=ACT.Square, bias=negmean, scale=1.0, accum_out=sst[:, m, 4:5])

        def st2(m):
            negmean = sst[:, m, 3:4]
            rstd = sst[:, m, 5:6]
            a = sst[:, m, 6:7]
            r1 = sst[:, m, 7:8]
            nc.scalar.activation(out=rstd, in_=sst[:, m, 4:5], func=RSFUNC, bias=epscol[:, 0:1], scale=1.0 / N)
            nc.scalar.activation(out=a, in_=negmean, func=ACT.Copy, scale=rstd)
            nc.scalar.activation(out=lm[m][:, 0:1], in_=negmean, func=ACT.Copy, scale=rstd)
            nc.scalar.activation(out=r1, in_=lm[m][:, 0:1], func=ACT.Identity, scale=-1.0, bias=a)
            nc.scalar.activation(out=lm[m][:, 1:2], in_=lm[m][:, 0:1], func=ACT.Identity, scale=-1.0, bias=a)
            nc.scalar.activation(out=lm[m][:, 2:3], in_=lm[m][:, 1:2], func=ACT.Identity, scale=-1.0, bias=r1)

        lt_ps = {}
        lt_sb = {}
        r_ps = {}
        o = {}

        def pt(m):
            if m == 0:
                lt_ps[0] = bank(5, [P, NB, P], BF16)
            nc.tensor.transpose(lt_ps[0][:, m, :], lm[m][:], ident_b[:])

        def sl(m):
            lt_sb[m] = keep.tile([P, P], BF16, name="lt_sb%d" % m)
            nc.vector.tensor_copy(out=lt_sb[m][:], in_=lt_ps[0][:, m, :])

        def pr(m, c):
            r_ps[(m, c)] = bank(RB[(3 * m + c) % 3], [P, CW], F32)
            nc.tensor.matmul(out=r_ps[(m, c)][:], lhsT=lt_sb[m][:], rhs=xrows[:, cols(c)], start=True, stop=True)

        def bb(m, c):
            if c == 0:
                o[m] = op.tile([P, N], F32, name="o")
            nc.vector.scalar_tensor_tensor(out=o[m][:, cols(c)], in0=yg[m][:, cols(c)], scalar=sst[:, m, 5:6], in1=r_ps[(m, c)][:], op0=ALU.mult, op1=ALU.add)
            nc.sync.dma_start(out=out_0[m][:, cols(c)], in_=o[m][:, cols(c)])

        def ca(m):
            nc.vector.tensor_reduce(out=vst[:, m, 0:1], in_=o[m][:], axis=AX.X, op=ALU.max, apply_absolute_value=True)

        def rc(m):
            nc.vector.reciprocal(out=vst[:, m, 1:2], in_=vst[:, m, 0:1])

        def rr(m):
            nc.scalar.activation(out=sca[:, m:m + 1], in_=vst[:, m, 1:2], func=ACT.Copy, scale=448.0)

        def rrv(m):
            nc.vector.tensor_scalar(out=sca[:, m:m + 1], in0=vst[:, m, 1:2], scalar1=448.0, scalar2=None, op0=ALU.mult)

        def kk(m, split):
            o8 = work.tile([P, N], FP8, name="o8")
            if split < N:
                nc.vector.tensor_scalar(out=o8[:, split:N], in0=o[m][:, split:N], scalar1=sca[:, m:m + 1], scalar2=None, op0=ALU.mult, saturate=False)
            nc.scalar.activation(out=o8[:, 0:split], in_=o[m][:, 0:split], func=ACT.Identity, scale=sca[:, m:m + 1], bias=zcol[:, 0:1], saturate=False)
            nc.sync.dma_start(out=out_1[m], in_=o8[:].bitcast(U8))

        rw = {}
        rx = {}
        rw[0] = run_w(0, True)
        qw(rw[0], 0)
        spread()
        rx[0] = run_x(0)
        p0(0, 0, CW)
        qx(rx[0], 0)
        rw[1] = run_w(1)
        mm(0, 0)
        mm(0, 1)
        p0(0, CW, N)
        p0(1, 0, CW)
        qw(rw[1], 1)
        rw[2] = run_w(2)
        mm(1, 0)
        mm(1, 1)
        p0(1, CW, N)
        qw(rw[2], 2)
        p1(0, 0)
        rw[3] = run_w(3)
        mm(2, 0)
        mm(2, 1)
        p0(2, 0, N)
        qw(rw[3], 3)
        rw[4] = run_w(4)
        mm(3, 0)
        mm(3, 1)
        p0(3, 0, 2 * CW)
        qw(rw[4], 4)
        p1(0, 1)
        rw[5] = run_w(5)
        mm(4, 0)
        p0(3, 2 * CW, N)
        qw(rw[5], 5)
        rx[1] = run_x(1, (0, 1))
        mm(5, 0)
        run_x(1, (2,), rx[1])
        p1(0, 2)
        st1(0)
        st2(0)
        p1(1, 0)
        qx(rx[1], 1)
        mm(4, 1)
        mm(5, 1)
        p1(1, 1)
        p1(1, 2)
        p2(1, 1)
        for c in (2, 0, 1):
            p2(0, c)
        p2(1, 0)
        p2(1, 2)
        st1(1)
        st2(1)
        for q in range(6):
            mm(q, 2)
        mm(0, 3)
        mm(1, 3)
        pt(0)
        for c in range(3):
            p1(2, c)
        st1(2)
        st2(2)
        for c in range(3):
            p2(2, c)
        sl(0)
        for q in range(2, 6):
            mm(q, 3)
        for c in range(3):
            p1(3, c)
        st1(3)
        st2(3)
        for c in range(3):
            p2(3, c)
        for c in range(3):
            pr(0, c)
        pt(1)
        bb(0, 0)
        bb(0, 1)
        sl(1)
        bb(0, 2)
        for c in range(3):
            pr(1, c)
        pt(2)
        bb(1, 0)
        ca(0)
        sl(2)
        bb(1, 1)
        rc(0)
        bb(1, 2)
        for c in range(3):
            pr(2, c)
        pt(3)
        rr(0)
        kk(0, N)
        bb(2, 0)
        ca(1)
        sl(3)
        bb(2, 1)
        rc(1)
        bb(2, 2)
        rr(1)
        kk(1, N)
        for c in range(3):
            pr(3, c)
        bb(3, 0)
        ca(2)
        bb(3, 1)
        rc(2)
        bb(3, 2)
        rr(2)
        kk(2, N)
        ca(3)
        rc(3)
        rrv(3)
        kk(3, CW)
